import numpy as np
import ml_dtypes


def mxq(x, axis, fmt="e4m3"):
    dtype, down = {"e4m3": (ml_dtypes.float8_e4m3fn, 7), "e5m2": (ml_dtypes.float8_e5m2, 14)}[fmt]
    v = np.moveaxis(np.asarray(x, np.float32).astype(ml_dtypes.bfloat16).astype(np.float64), axis, -1)
    blocks = v.reshape(v.shape[:-1] + (-1, 32))
    amax = np.abs(blocks).max(-1, keepdims=True)
    byte = np.maximum(np.where(amax > 0, np.frexp(amax)[1] - 1 + 127, 0) - down, 1)
    scale = np.exp2(byte - 127.0)
    codes = (blocks / scale).astype(np.float32).astype(dtype).astype(np.float64)
    return np.moveaxis((codes * scale).reshape(v.shape), -1, axis)


WIDE = False


def mx_kscale(k):
    if not WIDE:
        return np.ones(k)
    levels = np.array([10, -10, 5, -5, 0])
    a = np.random.permutation(np.resize(levels, k // 512 * 4)).reshape(k // 512, 4)
    idx = np.arange(k)
    return np.exp2(a[idx // 512, idx % 128 // 32])


BF16 = ml_dtypes.bfloat16


def bf(x):
    return np.asarray(x, np.float32).astype(BF16)


def f64(x):
    return np.asarray(x).astype(np.float64)


B, CK, CV, NOBJ, T, H, W = 4, 128, 256, 2, 1, 32, 32
N = T * H * W
P = H * W
V = NOBJ * CV


def setup_inputs():
    s = mx_kscale(N)
    a = np.log2(s) - np.log2(s).min()
    g = np.exp2(np.round(np.log2(np.mean(1.0 / s))))
    ms = bf(1.0 + 0.5 * np.random.random((B, T, H, W)))[:, None]
    qe = np.random.random((B, CK, H, W))
    qe[:, 0] = 1.0
    m2 = np.random.standard_normal((B, CK, T, H, W)) ** 2
    m2[:, 0] += (a * np.log(2.0) * np.sqrt(CK)).reshape(T, H, W) / f64(ms)[:, 0]
    return {
        "query_key": bf(np.random.standard_normal((B, CK, H, W))),
        "query_selection": bf(qe),
        "qk_sel": bf(np.random.standard_normal((B, CK, H, W)) * np.random.random((B, CK, H, W))),
        "memory_key": bf(np.random.standard_normal((B, CK, T, H, W))),
        "mk_sq": bf(m2),
        "memory_shrinkage": ms,
        "memory_value": bf(2.0 * np.random.standard_normal((B, NOBJ, CV, T, H, W)) * (s * g).reshape(T, H, W)),
    }


def reference(query_key, query_selection, qk_sel, memory_key, mk_sq, memory_shrinkage, memory_value):
    qk = f64(query_key).reshape(B, CK, P)
    qe = f64(query_selection).reshape(B, CK, P)
    qs = f64(qk_sel).reshape(B, CK, P)
    mk = f64(memory_key).reshape(B, CK, N)
    m2 = f64(mk_sq).reshape(B, CK, N)
    ms = f64(memory_shrinkage).reshape(B, N)
    mv = f64(memory_value).reshape(B, V, N)
    a_sq = m2.transpose(0, 2, 1) @ qe
    two_ab = 2.0 * (mk.transpose(0, 2, 1) @ qs)
    b_sq = np.sum(qe * qk * qk, axis=1, keepdims=True)
    sim = (two_ab - a_sq - b_sq) * ms[:, :, None] * (1.0 / np.sqrt(CK))
    e = np.exp(sim - sim.max(axis=1, keepdims=True))
    mem = (mxq(mv, 2, "e4m3") @ mxq(e, 1, "e4m3")) / e.sum(axis=1, keepdims=True)
    return mem.reshape(B, NOBJ, CV, H, W)

@@ -1,0 +1,211 @@
+import math
+from contextlib import ExitStack
+
+import concourse.mybir as mybir
+from concourse.masks import make_identity
+
+F32 = mybir.dt.float32
+BF16 = mybir.dt.bfloat16
+U32 = mybir.dt.uint32
+U8 = mybir.dt.uint8
+FP8X4 = mybir.dt.float8_e4m3fn_x4
+ALU = mybir.AluOpType
+ACT = mybir.ActivationFunctionType
+AXIS = mybir.AxisListType
+
+BATCH = 4
+P = 128
+SLOTS = 1024
+PIXELS = 1024
+VALUES = 512
+BANK = 512
+PACK = 4
+K_PASS = P * PACK
+PASSES = SLOTS // K_PASS
+ROW_TILES = PIXELS // P
+HALF_TILES = BANK // P
+HALVES = PIXELS // BANK
+V_TILES = VALUES // P
+PREPARE_AT = 2
+
+FLOPS = 2 * BATCH * (2 * P * SLOTS * PIXELS + VALUES * SLOTS * PIXELS)
+
+
+def tile_xmem_pa_t_kernel(
+    tc,
+    query_key,
+    query_selection,
+    qk_sel,
+    memory_key,
+    mk_sq,
+    memory_shrinkage,
+    memory_value,
+    out,
+):
+    nc = tc.nc
+    with ExitStack() as ctx:
+        consts = ctx.enter_context(tc.tile_pool(name="consts", bufs=1))
+        inputs = ctx.enter_context(tc.tile_pool(name="inputs", bufs=BATCH))
+        prep = ctx.enter_context(tc.tile_pool(name="prep", bufs=2))
+        rows = ctx.enter_context(tc.tile_pool(name="rows", bufs=3))
+        halves = ctx.enter_context(tc.tile_pool(name="halves", bufs=2))
+        results = ctx.enter_context(tc.tile_pool(name="results", bufs=4))
+        psum_sim = ctx.enter_context(tc.psum_pool(name="psum_sim", bufs=4))
+        psum_turn = ctx.enter_context(tc.psum_pool(name="psum_turn", bufs=2))
+        psum_out = ctx.enter_context(tc.psum_pool(name="psum_out", bufs=2))
+
+        loaded = []
+        for b in range(BATCH):
+            qk = inputs.tile([P, PIXELS], BF16)
+            nc.sync.dma_start(out=qk[:], in_=query_key[b].rearrange("c h w -> c (h w)"))
+            qe = inputs.tile([P, PIXELS], BF16)
+            nc.sync.dma_start(out=qe[:], in_=query_selection[b].rearrange("c h w -> c (h w)"))
+            ms_rows = inputs.tile([P, SLOTS], BF16)
+            nc.scalar.dma_start(
+                out=ms_rows[:],
+                in_=memory_shrinkage[b].rearrange("a t h w -> (a t h w)").partition_broadcast(P),
+            )
+            qs = inputs.tile([P, PIXELS], BF16)
+            nc.sync.dma_start(out=qs[:], in_=qk_sel[b].rearrange("c h w -> c (h w)"))
+            mk = inputs.tile([P, SLOTS], BF16)
+            nc.sync.dma_start(out=mk[:], in_=memory_key[b].rearrange("c t h w -> c (t h w)"))
+            m2 = inputs.tile([P, SLOTS], BF16)
+            nc.sync.dma_start(out=m2[:], in_=mk_sq[b].rearrange("c t h w -> c (t h w)"))
+            mv = inputs.tile([P, V_TILES, SLOTS], BF16)
+            nc.sync.dma_start(
+                out=mv[:],
+                in_=memory_value[b].rearrange("o c t h w -> (o c) (t h w)").rearrange(
+                    "(j q) n -> q j n", q=P
+                ),
+            )
+            loaded.append({"qk": qk, "qe": qe, "ms_rows": ms_rows, "qs": qs, "mk": mk, "m2": m2, "mv": mv})
+
+        ident = consts.tile([P, P], F32)
+        make_identity(nc, ident[:])
+        ones_square = consts.tile([P, P], F32)
+        nc.gpsimd.memset(ones_square[:], 1.0)
+        ones_column = consts.tile([P, 1], F32)
+        nc.gpsimd.memset(ones_column[:], 1.0)
+
+        def to_contraction_layout(rows_bf16, grouped, first_col):
+            words = rows_bf16.bitcast(F32)
+            turned = psum_turn.tile([P, PASSES * 2, P], F32, tag="turned")
+            for k in range(PASSES * 2):
+                nc.tensor.transpose(
+                    out=turned[:, k, :], in_=words[:, k * P : (k + 1) * P], identity=ident[:]
+                )
+            nc.scalar.copy(
+                out=grouped.bitcast(F32).rearrange("q (g r u) -> q g r u", g=PASSES, u=2)[
+                    :, :, first_col : first_col + P, :
+                ],
+                in_=turned[:].rearrange("q (g u) r -> q g r u", g=PASSES),
+            )
+
+        def prepare(b):
+            src = loaded[b]
+            qs2 = prep.tile([P, PIXELS], BF16)
+            nc.vector.tensor_scalar(out=qs2[:], in0=src["qs"][:], scalar1=2.0, scalar2=None, op0=ALU.mult)
+            qe_neg = prep.tile([P, PIXELS], BF16)
+            nc.vector.tensor_scalar(out=qe_neg[:], in0=src["qe"][:], scalar1=-1.0, scalar2=None, op0=ALU.mult)
+            weighted = prep.tile([P, PIXELS], F32)
+            nc.gpsimd.tensor_tensor(out=weighted[:], in0=src["qk"][:], in1=src["qk"][:], op=ALU.mult)
+            nc.gpsimd.tensor_tensor(out=weighted[:], in0=weighted[:], in1=src["qe"][:], op=ALU.mult)
+            neg_ms = prep.tile([P, SLOTS], F32)
+            nc.gpsimd.tensor_scalar(
+                out=neg_ms[:], in0=src["ms_rows"][:], scalar1=-1.0 / math.sqrt(P), scalar2=0.0,
+                op0=ALU.mult, op1=ALU.add,
+            )
+            b_sq_psum = psum_turn.tile([P, ROW_TILES], F32, tag="turned")
+            for i in range(ROW_TILES):
+                nc.tensor.matmul(
+                    out=b_sq_psum[:, i : i + 1], lhsT=weighted[:, i * P : (i + 1) * P], rhs=ones_column[:],
+                    start=True, stop=True,
+                )
+            b_sq = prep.tile([P, ROW_TILES], F32)
+            nc.vector.tensor_copy(out=b_sq[:], in_=b_sq_psum[:])
+
+            mv_grouped = prep.tile([P, PASSES * VALUES * PACK], BF16, align_bytes=64)
+            for j in range(V_TILES):
+                to_contraction_layout(src["mv"][:, j, :], mv_grouped[:], j * P)
+            mv_codes = prep.tile([P, PASSES * VALUES], U32, align_bytes=64)
+            mv_scales = prep.tile([P, PASSES * VALUES], U8, align_bytes=64)
+            nc.vector.quantize_mx(out=mv_codes[:].bitcast(FP8X4), scales=mv_scales[:], in_=mv_grouped[:])
+            return {
+                "qs2": qs2, "qe_neg": qe_neg, "neg_ms": neg_ms, "b_sq": b_sq,
+                "mv_codes": mv_codes, "mv_scales": mv_scales, "mk": src["mk"], "m2": src["m2"],
+            }
+
+        def softmax_rows(ops, i, e_grouped, sums, j):
+            pix = slice(i * P, (i + 1) * P)
+            neg_sim = rows.tile([P, SLOTS], F32)
+            for h in range(SLOTS // BANK):
+                cols = slice(h * BANK, (h + 1) * BANK)
+                dots = psum_sim.tile([P, BANK], F32)
+                nc.tensor.matmul(out=dots[:], lhsT=ops["qs2"][:, pix], rhs=ops["mk"][:, cols], start=True, stop=False)
+                nc.tensor.matmul(out=dots[:], lhsT=ops["qe_neg"][:, pix], rhs=ops["m2"][:, cols], start=False, stop=True)
+                nc.vector.scalar_tensor_tensor(
+                    out=neg_sim[:, cols], in0=dots[:], scalar=ops["b_sq"][:, i : i + 1], in1=ops["neg_ms"][:, cols],
+                    op0=ALU.subtract, op1=ALU.mult,
+                )
+            neg_max = rows.tile([P, 1], F32)
+            nc.vector.tensor_reduce(out=neg_max[:], in_=neg_sim[:], axis=AXIS.X, op=ALU.min)
+            e_rows = rows.tile([P, SLOTS], BF16)
+            nc.scalar.activation(
+                out=e_rows[:], in_=neg_sim[:], func=ACT.Exp, bias=neg_max[:], scale=-1.0,
+                accum_out=sums[:, j : j + 1],
+            )
+            to_contraction_layout(e_rows[:], e_grouped[:], j * P)
+
+        def readout(b, ops, half, e_grouped, sums):
+            e_codes = halves.tile([P, PASSES * BANK], U32, align_bytes=64)
+            e_scales = halves.tile([P, PASSES * BANK], U8, align_bytes=64)
+            nc.vector.quantize_mx(out=e_codes[:].bitcast(FP8X4), scales=e_scales[:], in_=e_grouped[:])
+
+            recip = halves.tile([P, HALF_TILES], F32)
+            nc.vector.reciprocal(out=recip[:], in_=sums[:])
+            spread = halves.tile([P, HALF_TILES, P], F32)
+            for j in range(HALF_TILES):
+                nc.gpsimd.tensor_scalar(
+                    out=spread[:, j, :], in0=ones_square[:], scalar1=recip[:, j : j + 1], scalar2=0.0,
+                    op0=ALU.mult, op1=ALU.add,
+                )
+            turned = psum_turn.tile([P, HALF_TILES, P], F32, tag="turned")
+            for j in range(HALF_TILES):
+                nc.tensor.transpose(out=turned[:, j, :], in_=spread[:, j, :], identity=ident[:])
+            recip_rows = halves.tile([P, BANK], F32)
+            nc.scalar.copy(out=recip_rows[:], in_=turned[:].rearrange("q j r -> q (j r)"))
+
+            out_b = out[b].rearrange("o c h w -> (o c) (h w)")
+            for j in range(V_TILES):
+                acc = psum_out.tile([P, BANK], F32)
+                for g in range(PASSES):
+                    v_cols = slice(g * VALUES + j * P, g * VALUES + (j + 1) * P)
+                    p_cols = slice(g * BANK, (g + 1) * BANK)
+                    nc.tensor.matmul_mx(
+                        out=acc[:],
+                        lhsT=ops["mv_codes"][:, v_cols].bitcast(FP8X4),
+                        lhsT_scale=ops["mv_scales"][:, v_cols],
+                        rhs=e_codes[:, p_cols].bitcast(FP8X4),
+                        rhs_scale=e_scales[:, p_cols],
+                        start=(g == 0),
+                        stop=(g == PASSES - 1),
+                    )
+                result = results.tile([P, BANK], F32)
+                nc.scalar.copy(out=result[:], in_=acc[:])
+                nc.gpsimd.tensor_tensor(out=result[:], in0=result[:], in1=recip_rows[:], op=ALU.mult)
+                nc.sync.dma_start(
+                    out=out_b[j * P : (j + 1) * P, half * BANK : (half + 1) * BANK], in_=result[:]
+                )
+
+        ops_next = prepare(0)
+        for b in range(BATCH):
+            ops = ops_next
+            for half in range(HALVES):
+                e_grouped = halves.tile([P, PASSES * BANK * PACK], BF16, align_bytes=64)
+                sums = halves.tile([P, HALF_TILES], F32)
+                for j in range(HALF_TILES):
+                    i = half * HALF_TILES + j
+                    if i == PREPARE_AT and b + 1 < BATCH:
+                        ops_next = prepare(b + 1)
+                    softmax_rows(ops, i, e_grouped, sums, j)
+                readout(b, ops, half, e_grouped, sums)

@@ -24,9 +24,9 @@ K_PASS = P * PACK
 PASSES = SLOTS // K_PASS
 ROW_TILES = PIXELS // P
 HALF_TILES = BANK // P
-HALVES = PIXELS // BANK
 V_TILES = VALUES // P
-PREPARE_AT = 2
+TILES = BATCH * ROW_TILES
+HALVES = TILES // HALF_TILES
 
 FLOPS = 2 * BATCH * (2 * P * SLOTS * PIXELS + VALUES * SLOTS * PIXELS)
 
@@ -49,12 +49,14 @@ def tile_xmem_pa_t_kernel(
         prep = ctx.enter_context(tc.tile_pool(name="prep", bufs=2))
         rows = ctx.enter_context(tc.tile_pool(name="rows", bufs=3))
         halves = ctx.enter_context(tc.tile_pool(name="halves", bufs=2))
-        results = ctx.enter_context(tc.tile_pool(name="results", bufs=4))
+        results = ctx.enter_context(tc.tile_pool(name="results", bufs=6))
         psum_sim = ctx.enter_context(tc.psum_pool(name="psum_sim", bufs=4))
-        psum_turn = ctx.enter_context(tc.psum_pool(name="psum_turn", bufs=2))
-        psum_out = ctx.enter_context(tc.psum_pool(name="psum_out", bufs=2))
+        psum_e = ctx.enter_context(tc.psum_pool(name="psum_e", bufs=2))
+        psum_small = ctx.enter_context(tc.psum_pool(name="psum_small", bufs=2))
+        ctx.enter_context(tc.manual_schedule())
 
-        loaded = []
+        live = {}
+
         for b in range(BATCH):
             qk = inputs.tile([P, PIXELS], BF16)
             nc.sync.dma_start(out=qk[:], in_=query_key[b].rearrange("c h w -> c (h w)"))
@@ -78,134 +80,249 @@ def tile_xmem_pa_t_kernel(
                     "(j q) n -> q j n", q=P
                 ),
             )
-            loaded.append({"qk": qk, "qe": qe, "ms_rows": ms_rows, "qs": qs, "mk": mk, "m2": m2, "mv": mv})
+            live["qk", b], live["qe", b], live["ms_rows", b], live["qs", b] = qk, qe, ms_rows, qs
+            live["mk", b], live["m2", b], live["mv", b] = mk, m2, mv
 
         ident = consts.tile([P, P], F32)
         make_identity(nc, ident[:])
-        ones_square = consts.tile([P, P], F32)
-        nc.gpsimd.memset(ones_square[:], 1.0)
         ones_column = consts.tile([P, 1], F32)
         nc.gpsimd.memset(ones_column[:], 1.0)
 
-        def to_contraction_layout(rows_bf16, grouped, first_col):
+        def square_keys(b, engine):
+            weighted = prep.tile([P, PIXELS], F32)
+            engine.tensor_tensor(out=weighted[:], in0=live["qk", b][:], in1=live["qk", b][:], op=ALU.mult)
+            live["weighted", b] = weighted
+
+        def weight_squares(b, engine):
+            weighted = live["weighted", b]
+            engine.tensor_tensor(out=weighted[:], in0=weighted[:], in1=live["qe", b][:], op=ALU.mult)
+
+        def scale_queries(b, engine):
+            qs2 = prep.tile([P, PIXELS], BF16)
+            engine.tensor_scalar(
+                out=qs2[:], in0=live["qs", b][:], scalar1=2.0, scalar2=0.0, op0=ALU.mult, op1=ALU.add
+            )
+            qe_neg = prep.tile([P, PIXELS], BF16)
+            engine.tensor_scalar(
+                out=qe_neg[:], in0=live["qe", b][:], scalar1=-1.0, scalar2=0.0, op0=ALU.mult, op1=ALU.add
+            )
+            live["qs2", b], live["qe_neg", b] = qs2, qe_neg
+
+        def scale_shrinkage(b, engine):
+            neg_ms = prep.tile([P, SLOTS], F32)
+            engine.tensor_scalar(
+                out=neg_ms[:], in0=live["ms_rows", b][:], scalar1=-1.0 / math.sqrt(P), scalar2=0.0,
+                op0=ALU.mult, op1=ALU.add,
+            )
+            live["neg_ms", b] = neg_ms
+
+        def channel_sums(b):
+            b_sq_psum = psum_small.tile([P, ROW_TILES], F32, tag="small")
+            for i in range(ROW_TILES):
+                nc.tensor.matmul(
+                    out=b_sq_psum[:, i : i + 1], lhsT=live["weighted", b][:, i * P : (i + 1) * P],
+                    rhs=ones_column[:], start=True, stop=True,
+                )
+            live["b_sq_psum", b] = b_sq_psum
+
+        def keep_channel_sums(b):
+            b_sq = prep.tile([P, ROW_TILES], F32)
+            nc.vector.tensor_copy(out=b_sq[:], in_=live["b_sq_psum", b][:])
+            live["b_sq", b] = b_sq
+
+        def turn_words(rows_bf16, turned):
             words = rows_bf16.bitcast(F32)
-            turned = psum_turn.tile([P, PASSES * 2, P], F32, tag="turned")
             for k in range(PASSES * 2):
                 nc.tensor.transpose(
                     out=turned[:, k, :], in_=words[:, k * P : (k + 1) * P], identity=ident[:]
                 )
+
+        def regroup_words(turned, grouped, first_col):
             nc.scalar.copy(
-                out=grouped.bitcast(F32).rearrange("q (g r u) -> q g r u", g=PASSES, u=2)[
+                out=grouped[:].bitcast(F32).rearrange("q (g r u) -> q g r u", g=PASSES, u=2)[
                     :, :, first_col : first_col + P, :
                 ],
                 in_=turned[:].rearrange("q (g u) r -> q g r u", g=PASSES),
             )
 
-        def prepare(b):
-            src = loaded[b]
-            qs2 = prep.tile([P, PIXELS], BF16)
-            nc.vector.tensor_scalar(out=qs2[:], in0=src["qs"][:], scalar1=2.0, scalar2=None, op0=ALU.mult)
-            qe_neg = prep.tile([P, PIXELS], BF16)
-            nc.vector.tensor_scalar(out=qe_neg[:], in0=src["qe"][:], scalar1=-1.0, scalar2=None, op0=ALU.mult)
-            weighted = prep.tile([P, PIXELS], F32)
-            nc.gpsimd.tensor_tensor(out=weighted[:], in0=src["qk"][:], in1=src["qk"][:], op=ALU.mult)
-            nc.gpsimd.tensor_tensor(out=weighted[:], in0=weighted[:], in1=src["qe"][:], op=ALU.mult)
-            neg_ms = prep.tile([P, SLOTS], F32)
-            nc.gpsimd.tensor_scalar(
-                out=neg_ms[:], in0=src["ms_rows"][:], scalar1=-1.0 / math.sqrt(P), scalar2=0.0,
-                op0=ALU.mult, op1=ALU.add,
-            )
-            b_sq_psum = psum_turn.tile([P, ROW_TILES], F32, tag="turned")
-            for i in range(ROW_TILES):
-                nc.tensor.matmul(
-                    out=b_sq_psum[:, i : i + 1], lhsT=weighted[:, i * P : (i + 1) * P], rhs=ones_column[:],
-                    start=True, stop=True,
-                )
-            b_sq = prep.tile([P, ROW_TILES], F32)
-            nc.vector.tensor_copy(out=b_sq[:], in_=b_sq_psum[:])
+        def turn_values(b, j):
+            if not (0 <= b < BATCH and j < V_TILES):
+                return
+            mv_turned = psum_small.tile([P, PASSES * 2, P], F32, tag="small")
+            turn_words(live["mv", b][:, j, :], mv_turned)
+            live["mv_turned", b, j] = mv_turned
 
-            mv_grouped = prep.tile([P, PASSES * VALUES * PACK], BF16, align_bytes=64)
-            for j in range(V_TILES):
-                to_contraction_layout(src["mv"][:, j, :], mv_grouped[:], j * P)
+        def regroup_values(b, j):
+            if not (0 <= b < BATCH and j < V_TILES):
+                return
+            if j == 0:
+                mv_grouped = prep.tile([P, PASSES * VALUES * PACK], BF16, align_bytes=64, bufs=1)
+                live["mv_grouped", b] = mv_grouped
+            regroup_words(live["mv_turned", b, j], live["mv_grouped", b], j * P)
+
+        def quantise_values(b):
             mv_codes = prep.tile([P, PASSES * VALUES], U32, align_bytes=64)
             mv_scales = prep.tile([P, PASSES * VALUES], U8, align_bytes=64)
-            nc.vector.quantize_mx(out=mv_codes[:].bitcast(FP8X4), scales=mv_scales[:], in_=mv_grouped[:])
-            return {
-                "qs2": qs2, "qe_neg": qe_neg, "neg_ms": neg_ms, "b_sq": b_sq,
-                "mv_codes": mv_codes, "mv_scales": mv_scales, "mk": src["mk"], "m2": src["m2"],
-            }
+            nc.vector.quantize_mx(
+                out=mv_codes[:].bitcast(FP8X4), scales=mv_scales[:], in_=live["mv_grouped", b][:]
+            )
+            live["mv_codes", b], live["mv_scales", b] = mv_codes, mv_scales
 
-        def softmax_rows(ops, i, e_grouped, sums, j):
-            pix = slice(i * P, (i + 1) * P)
-            neg_sim = rows.tile([P, SLOTS], F32)
-            for h in range(SLOTS // BANK):
-                cols = slice(h * BANK, (h + 1) * BANK)
+        def similarities(i):
+            if not 0 <= i < TILES:
+                return
+            b, t = divmod(i, ROW_TILES)
+            pix = slice(t * P, (t + 1) * P)
+            for c in range(SLOTS // BANK):
+                cols = slice(c * BANK, (c + 1) * BANK)
                 dots = psum_sim.tile([P, BANK], F32)
-                nc.tensor.matmul(out=dots[:], lhsT=ops["qs2"][:, pix], rhs=ops["mk"][:, cols], start=True, stop=False)
-                nc.tensor.matmul(out=dots[:], lhsT=ops["qe_neg"][:, pix], rhs=ops["m2"][:, cols], start=False, stop=True)
+                nc.tensor.matmul(
+                    out=dots[:], lhsT=live["qs2", b][:, pix], rhs=live["mk", b][:, cols], start=True, stop=False
+                )
+                nc.tensor.matmul(
+                    out=dots[:], lhsT=live["qe_neg", b][:, pix], rhs=live["m2", b][:, cols], start=False, stop=True
+                )
+                live["dots", i, c] = dots
+
+        def negated_similarities(i):
+            if not 0 <= i < TILES:
+                return
+            b, t = divmod(i, ROW_TILES)
+            neg_sim = rows.tile([P, SLOTS], F32)
+            for c in range(SLOTS // BANK):
+                cols = slice(c * BANK, (c + 1) * BANK)
                 nc.vector.scalar_tensor_tensor(
-                    out=neg_sim[:, cols], in0=dots[:], scalar=ops["b_sq"][:, i : i + 1], in1=ops["neg_ms"][:, cols],
-                    op0=ALU.subtract, op1=ALU.mult,
+                    out=neg_sim[:, cols], in0=live["dots", i, c][:], scalar=live["b_sq", b][:, t : t + 1],
+                    in1=live["neg_ms", b][:, cols], op0=ALU.subtract, op1=ALU.mult,
                 )
             neg_max = rows.tile([P, 1], F32)
             nc.vector.tensor_reduce(out=neg_max[:], in_=neg_sim[:], axis=AXIS.X, op=ALU.min)
+            live["neg_sim", i], live["neg_max", i] = neg_sim, neg_max
+
+        def exponentials(i):
+            if not 0 <= i < TILES:
+                return
+            h, j = divmod(i, HALF_TILES)
+            if j == 0:
+                sums = halves.tile([P, HALF_TILES], F32)
+                live["sums", h] = sums
             e_rows = rows.tile([P, SLOTS], BF16)
             nc.scalar.activation(
-                out=e_rows[:], in_=neg_sim[:], func=ACT.Exp, bias=neg_max[:], scale=-1.0,
-                accum_out=sums[:, j : j + 1],
+                out=e_rows[:], in_=live["neg_sim", i][:], func=ACT.Exp, bias=live["neg_max", i][:], scale=-1.0,
+                accum_out=live["sums", h][:, j : j + 1],
             )
-            to_contraction_layout(e_rows[:], e_grouped[:], j * P)
+            live["e_rows", i] = e_rows
 
-        def readout(b, ops, half, e_grouped, sums):
+        def turn_e(i):
+            if not 0 <= i < TILES:
+                return
+            e_turned = psum_e.tile([P, PASSES * 2, P], F32)
+            turn_words(live["e_rows", i][:], e_turned)
+            live["e_turned", i] = e_turned
+
+        def regroup_e(i):
+            if not 0 <= i < TILES:
+                return
+            h, j = divmod(i, HALF_TILES)
+            if j == 0:
+                e_grouped = halves.tile([P, PASSES * BANK * PACK], BF16, align_bytes=64)
+                live["e_grouped", h] = e_grouped
+            regroup_words(live["e_turned", i], live["e_grouped", h], j * P)
+
+        def reciprocals(h):
+            recip = halves.tile([P, HALF_TILES], F32)
+            nc.vector.reciprocal(out=recip[:], in_=live["sums", h][:])
+            live["recip", h] = recip
+
+        def spread_reciprocals(h):
+            recip_spread = psum_small.tile([P, BANK], F32, tag="small")
+            for j in range(HALF_TILES):
+                nc.tensor.matmul(
+                    out=recip_spread[:, j * P : (j + 1) * P],
+                    lhsT=live["recip", h][:, j : j + 1].to_broadcast([P, P]),
+                    rhs=ident[:],
+                    start=True,
+                    stop=True,
+                )
+            live["recip_spread", h] = recip_spread
+
+        def keep_reciprocals(h):
+            recip_rows = halves.tile([P, BANK], F32)
+            nc.scalar.copy(out=recip_rows[:], in_=live["recip_spread", h][:])
+            live["recip_rows", h] = recip_rows
+
+        def quantise_e(h):
             e_codes = halves.tile([P, PASSES * BANK], U32, align_bytes=64)
             e_scales = halves.tile([P, PASSES * BANK], U8, align_bytes=64)
-            nc.vector.quantize_mx(out=e_codes[:].bitcast(FP8X4), scales=e_scales[:], in_=e_grouped[:])
+            nc.vector.quantize_mx(
+                out=e_codes[:].bitcast(FP8X4), scales=e_scales[:], in_=live["e_grouped", h][:]
+            )
+            live["e_codes", h], live["e_scales", h] = e_codes, e_scales
 
-            recip = halves.tile([P, HALF_TILES], F32)
-            nc.vector.reciprocal(out=recip[:], in_=sums[:])
-            spread = halves.tile([P, HALF_TILES, P], F32)
-            for j in range(HALF_TILES):
-                nc.gpsimd.tensor_scalar(
-                    out=spread[:, j, :], in0=ones_square[:], scalar1=recip[:, j : j + 1], scalar2=0.0,
-                    op0=ALU.mult, op1=ALU.add,
+        def multiply_values(h, j):
+            b = h // 2
+            acc = psum_small.tile([P, BANK], F32, tag="small")
+            for g in range(PASSES):
+                v_cols = slice(g * VALUES + j * P, g * VALUES + (j + 1) * P)
+                p_cols = slice(g * BANK, (g + 1) * BANK)
+                nc.tensor.matmul_mx(
+                    out=acc[:],
+                    lhsT=live["mv_codes", b][:, v_cols].bitcast(FP8X4),
+                    lhsT_scale=live["mv_scales", b][:, v_cols],
+                    rhs=live["e_codes", h][:, p_cols].bitcast(FP8X4),
+                    rhs_scale=live["e_scales", h][:, p_cols],
+                    start=(g == 0),
+                    stop=(g == PASSES - 1),
                 )
-            turned = psum_turn.tile([P, HALF_TILES, P], F32, tag="turned")
-            for j in range(HALF_TILES):
-                nc.tensor.transpose(out=turned[:, j, :], in_=spread[:, j, :], identity=ident[:])
-            recip_rows = halves.tile([P, BANK], F32)
-            nc.scalar.copy(out=recip_rows[:], in_=turned[:].rearrange("q j r -> q (j r)"))
-
-            out_b = out[b].rearrange("o c h w -> (o c) (h w)")
-            for j in range(V_TILES):
-                acc = psum_out.tile([P, BANK], F32)
-                for g in range(PASSES):
-                    v_cols = slice(g * VALUES + j * P, g * VALUES + (j + 1) * P)
-                    p_cols = slice(g * BANK, (g + 1) * BANK)
-                    nc.tensor.matmul_mx(
-                        out=acc[:],
-                        lhsT=ops["mv_codes"][:, v_cols].bitcast(FP8X4),
-                        lhsT_scale=ops["mv_scales"][:, v_cols],
-                        rhs=e_codes[:, p_cols].bitcast(FP8X4),
-                        rhs_scale=e_scales[:, p_cols],
-                        start=(g == 0),
-                        stop=(g == PASSES - 1),
-                    )
-                result = results.tile([P, BANK], F32)
+            b, half = divmod(h, 2)
+            result = results.tile([P, BANK], F32)
+            if h == HALVES - 1:
+                nc.vector.tensor_tensor(out=result[:], in0=acc[:], in1=live["recip_rows", h][:], op=ALU.mult)
+            else:
                 nc.scalar.copy(out=result[:], in_=acc[:])
-                nc.gpsimd.tensor_tensor(out=result[:], in0=result[:], in1=recip_rows[:], op=ALU.mult)
-                nc.sync.dma_start(
-                    out=out_b[j * P : (j + 1) * P, half * BANK : (half + 1) * BANK], in_=result[:]
-                )
+                nc.gpsimd.tensor_tensor(out=result[:], in0=result[:], in1=live["recip_rows", h][:], op=ALU.mult)
+            nc.sync.dma_start(
+                out=out[b].rearrange("o c h w -> (o c) (h w)")[
+                    j * P : (j + 1) * P, half * BANK : (half + 1) * BANK
+                ],
+                in_=result[:],
+            )
 
-        ops_next = prepare(0)
-        for b in range(BATCH):
-            ops = ops_next
-            for half in range(HALVES):
-                e_grouped = halves.tile([P, PASSES * BANK * PACK], BF16, align_bytes=64)
-                sums = halves.tile([P, HALF_TILES], F32)
-                for j in range(HALF_TILES):
-                    i = half * HALF_TILES + j
-                    if i == PREPARE_AT and b + 1 < BATCH:
-                        ops_next = prepare(b + 1)
-                    softmax_rows(ops, i, e_grouped, sums, j)
-                readout(b, ops, half, e_grouped, sums)
+        for s in range(-ROW_TILES, TILES + 6):
+            b_next, step = divmod(s + ROW_TILES, ROW_TILES)
+            if b_next < BATCH:
+                engine = nc.vector if b_next == 0 else nc.gpsimd
+                if step == 0:
+                    square_keys(b_next, engine)
+                if step == 1:
+                    weight_squares(b_next, engine)
+                if step == 2:
+                    scale_queries(b_next, engine)
+                if step == 3:
+                    scale_shrinkage(b_next, engine)
+                if step == 4:
+                    channel_sums(b_next)
+
+            similarities(s + 2)
+            negated_similarities(s + 1)
+            exponentials(s)
+            regroup_e(s - 1)
+            regroup_values(s // ROW_TILES, s % ROW_TILES)
+            h, j = divmod(s - 6, V_TILES)
+            if 0 <= h < HALVES:
+                if j == 0:
+                    keep_reciprocals(h)
+                multiply_values(h, j)
+            turn_e(s)
+            if s % HALF_TILES == 1 and 0 <= (s - 5) // HALF_TILES < HALVES:
+                spread_reciprocals((s - 5) // HALF_TILES)
+            turn_values((s + 1) // ROW_TILES, (s + 1) % ROW_TILES)
+
+            if b_next < BATCH and step == 4:
+                keep_channel_sums(b_next)
+            if s % HALF_TILES == 0 and 0 <= (s - 4) // HALF_TILES < HALVES:
+                reciprocals((s - 4) // HALF_TILES)
+            if s % HALF_TILES == 1 and 0 <= (s - 5) // HALF_TILES < HALVES:
+                quantise_e((s - 5) // HALF_TILES)
+            if s % ROW_TILES == 4 and 0 <= s // ROW_TILES < BATCH:
+                quantise_values(s // ROW_TILES)

@@ -28,6 +28,8 @@ V_TILES = VALUES // P
 TILES = BATCH * ROW_TILES
 HALVES = TILES // HALF_TILES
 
+VECTOR_HALVES = 2
+
 FLOPS = 2 * BATCH * (2 * P * SLOTS * PIXELS + VALUES * SLOTS * PIXELS)
 
 
@@ -47,12 +49,12 @@ def tile_xmem_pa_t_kernel(
         consts = ctx.enter_context(tc.tile_pool(name="consts", bufs=1))
         inputs = ctx.enter_context(tc.tile_pool(name="inputs", bufs=BATCH))
         prep = ctx.enter_context(tc.tile_pool(name="prep", bufs=2))
-        rows = ctx.enter_context(tc.tile_pool(name="rows", bufs=3))
+        rows = ctx.enter_context(tc.tile_pool(name="rows", bufs=4))
         halves = ctx.enter_context(tc.tile_pool(name="halves", bufs=2))
         results = ctx.enter_context(tc.tile_pool(name="results", bufs=6))
-        psum_sim = ctx.enter_context(tc.psum_pool(name="psum_sim", bufs=4))
-        psum_e = ctx.enter_context(tc.psum_pool(name="psum_e", bufs=2))
-        psum_small = ctx.enter_context(tc.psum_pool(name="psum_small", bufs=2))
+        psum_wide = ctx.enter_context(tc.psum_pool(name="psum_wide", bufs=5))
+        psum_turn = ctx.enter_context(tc.psum_pool(name="psum_turn", bufs=2))
+        psum_misc = ctx.enter_context(tc.psum_pool(name="psum_misc", bufs=1))
         ctx.enter_context(tc.manual_schedule())
 
         live = {}
@@ -117,7 +119,9 @@ def tile_xmem_pa_t_kernel(
             live["neg_ms", b] = neg_ms
 
         def channel_sums(b):
-            b_sq_psum = psum_small.tile([P, ROW_TILES], F32, tag="small")
+            if not 0 <= b < BATCH:
+                return
+            b_sq_psum = psum_misc.tile([P, ROW_TILES], F32, tag="misc")
             for i in range(ROW_TILES):
                 nc.tensor.matmul(
                     out=b_sq_psum[:, i : i + 1], lhsT=live["weighted", b][:, i * P : (i + 1) * P],
@@ -126,6 +130,8 @@ def tile_xmem_pa_t_kernel(
             live["b_sq_psum", b] = b_sq_psum
 
         def keep_channel_sums(b):
+            if not 0 <= b < BATCH:
+                return
             b_sq = prep.tile([P, ROW_TILES], F32)
             nc.vector.tensor_copy(out=b_sq[:], in_=live["b_sq_psum", b][:])
             live["b_sq", b] = b_sq
@@ -148,7 +154,7 @@ def tile_xmem_pa_t_kernel(
         def turn_values(b, j):
             if not (0 <= b < BATCH and j < V_TILES):
                 return
-            mv_turned = psum_small.tile([P, PASSES * 2, P], F32, tag="small")
+            mv_turned = psum_turn.tile([P, PASSES * 2, P], F32, tag="turned")
             turn_words(live["mv", b][:, j, :], mv_turned)
             live["mv_turned", b, j] = mv_turned
 
@@ -161,6 +167,8 @@ def tile_xmem_pa_t_kernel(
             regroup_words(live["mv_turned", b, j], live["mv_grouped", b], j * P)
 
         def quantise_values(b):
+            if not 0 <= b < BATCH:
+                return
             mv_codes = prep.tile([P, PASSES * VALUES], U32, align_bytes=64)
             mv_scales = prep.tile([P, PASSES * VALUES], U8, align_bytes=64)
             nc.vector.quantize_mx(
@@ -168,36 +176,40 @@ def tile_xmem_pa_t_kernel(
             )
             live["mv_codes", b], live["mv_scales", b] = mv_codes, mv_scales
 
-        def similarities(i):
+        def similarities(i, c):
             if not 0 <= i < TILES:
                 return
             b, t = divmod(i, ROW_TILES)
             pix = slice(t * P, (t + 1) * P)
-            for c in range(SLOTS // BANK):
-                cols = slice(c * BANK, (c + 1) * BANK)
-                dots = psum_sim.tile([P, BANK], F32)
-                nc.tensor.matmul(
-                    out=dots[:], lhsT=live["qs2", b][:, pix], rhs=live["mk", b][:, cols], start=True, stop=False
-                )
-                nc.tensor.matmul(
-                    out=dots[:], lhsT=live["qe_neg", b][:, pix], rhs=live["m2", b][:, cols], start=False, stop=True
-                )
-                live["dots", i, c] = dots
+            cols = slice(c * BANK, (c + 1) * BANK)
+            dots = psum_wide.tile([P, BANK], F32, tag="wide")
+            nc.tensor.matmul(
+                out=dots[:], lhsT=live["qs2", b][:, pix], rhs=live["mk", b][:, cols], start=True, stop=False
+            )
+            nc.tensor.matmul(
+                out=dots[:], lhsT=live["qe_neg", b][:, pix], rhs=live["m2", b][:, cols], start=False, stop=True
+            )
+            live["dots", i, c] = dots
 
-        def negated_similarities(i):
+        def negated_similarities(i, c):
             if not 0 <= i < TILES:
                 return
             b, t = divmod(i, ROW_TILES)
-            neg_sim = rows.tile([P, SLOTS], F32)
-            for c in range(SLOTS // BANK):
-                cols = slice(c * BANK, (c + 1) * BANK)
-                nc.vector.scalar_tensor_tensor(
-                    out=neg_sim[:, cols], in0=live["dots", i, c][:], scalar=live["b_sq", b][:, t : t + 1],
-                    in1=live["neg_ms", b][:, cols], op0=ALU.subtract, op1=ALU.mult,
-                )
+            cols = slice(c * BANK, (c + 1) * BANK)
+            if c == 0:
+                neg_sim = rows.tile([P, SLOTS], F32)
+                live["neg_sim", i] = neg_sim
+            nc.vector.scalar_tensor_tensor(
+                out=live["neg_sim", i][:, cols], in0=live["dots", i, c][:], scalar=live["b_sq", b][:, t : t + 1],
+                in1=live["neg_ms", b][:, cols], op0=ALU.subtract, op1=ALU.mult,
+            )
+
+        def negated_maximum(i):
+            if not 0 <= i < TILES:
+                return
             neg_max = rows.tile([P, 1], F32)
-            nc.vector.tensor_reduce(out=neg_max[:], in_=neg_sim[:], axis=AXIS.X, op=ALU.min)
-            live["neg_sim", i], live["neg_max", i] = neg_sim, neg_max
+            nc.vector.tensor_reduce(out=neg_max[:], in_=live["neg_sim", i][:], axis=AXIS.X, op=ALU.min)
+            live["neg_max", i] = neg_max
 
         def exponentials(i):
             if not 0 <= i < TILES:
@@ -216,7 +228,7 @@ def tile_xmem_pa_t_kernel(
         def turn_e(i):
             if not 0 <= i < TILES:
                 return
-            e_turned = psum_e.tile([P, PASSES * 2, P], F32)
+            e_turned = psum_turn.tile([P, PASSES * 2, P], F32, tag="turned")
             turn_words(live["e_rows", i][:], e_turned)
             live["e_turned", i] = e_turned
 
@@ -230,12 +242,16 @@ def tile_xmem_pa_t_kernel(
             regroup_words(live["e_turned", i], live["e_grouped", h], j * P)
 
         def reciprocals(h):
+            if not 0 <= h < HALVES:
+                return
             recip = halves.tile([P, HALF_TILES], F32)
             nc.vector.reciprocal(out=recip[:], in_=live["sums", h][:])
             live["recip", h] = recip
 
         def spread_reciprocals(h):
-            recip_spread = psum_small.tile([P, BANK], F32, tag="small")
+            if not 0 <= h < HALVES:
+                return
+            recip_spread = psum_misc.tile([P, BANK], F32, tag="misc")
             for j in range(HALF_TILES):
                 nc.tensor.matmul(
                     out=recip_spread[:, j * P : (j + 1) * P],
@@ -247,11 +263,15 @@ def tile_xmem_pa_t_kernel(
             live["recip_spread", h] = recip_spread
 
         def keep_reciprocals(h):
+            if not 0 <= h < HALVES:
+                return
             recip_rows = halves.tile([P, BANK], F32)
             nc.scalar.copy(out=recip_rows[:], in_=live["recip_spread", h][:])
             live["recip_rows", h] = recip_rows
 
         def quantise_e(h):
+            if not 0 <= h < HALVES:
+                return
             e_codes = halves.tile([P, PASSES * BANK], U32, align_bytes=64)
             e_scales = halves.tile([P, PASSES * BANK], U8, align_bytes=64)
             nc.vector.quantize_mx(
@@ -260,8 +280,10 @@ def tile_xmem_pa_t_kernel(
             live["e_codes", h], live["e_scales", h] = e_codes, e_scales
 
         def multiply_values(h, j):
+            if not 0 <= h < HALVES:
+                return
             b = h // 2
-            acc = psum_small.tile([P, BANK], F32, tag="small")
+            acc = psum_wide.tile([P, BANK], F32, tag="wide")
             for g in range(PASSES):
                 v_cols = slice(g * VALUES + j * P, g * VALUES + (j + 1) * P)
                 p_cols = slice(g * BANK, (g + 1) * BANK)
@@ -274,13 +296,10 @@ def tile_xmem_pa_t_kernel(
                     start=(g == 0),
                     stop=(g == PASSES - 1),
                 )
+            live["acc", h, j] = acc
+
+        def store(h, j, result):
             b, half = divmod(h, 2)
-            result = results.tile([P, BANK], F32)
-            if h == HALVES - 1:
-                nc.vector.tensor_tensor(out=result[:], in0=acc[:], in1=live["recip_rows", h][:], op=ALU.mult)
-            else:
-                nc.scalar.copy(out=result[:], in_=acc[:])
-                nc.gpsimd.tensor_tensor(out=result[:], in0=result[:], in1=live["recip_rows", h][:], op=ALU.mult)
             nc.sync.dma_start(
                 out=out[b].rearrange("o c h w -> (o c) (h w)")[
                     j * P : (j + 1) * P, half * BANK : (half + 1) * BANK
@@ -288,8 +307,30 @@ def tile_xmem_pa_t_kernel(
                 in_=result[:],
             )
 
-        for s in range(-ROW_TILES, TILES + 6):
+        def leave_psum(h, j):
+            if not 0 <= h < HALVES:
+                return
+            result = results.tile([P, BANK], F32)
+            if h < HALVES - VECTOR_HALVES:
+                nc.scalar.copy(out=result[:], in_=live["acc", h, j][:])
+                live["result", h, j] = result
+            else:
+                nc.vector.tensor_tensor(
+                    out=result[:], in0=live["acc", h, j][:], in1=live["recip_rows", h][:], op=ALU.mult
+                )
+                store(h, j, result)
+
+        def normalise_and_store(h, j):
+            if not 0 <= h < HALVES - VECTOR_HALVES:
+                return
+            result = live["result", h, j]
+            nc.gpsimd.tensor_tensor(out=result[:], in0=result[:], in1=live["recip_rows", h][:], op=ALU.mult)
+            store(h, j, result)
+
+        for s in range(-ROW_TILES, TILES + 11):
             b_next, step = divmod(s + ROW_TILES, ROW_TILES)
+            h_now, quarter = divmod(s, HALF_TILES)
+
             if b_next < BATCH:
                 engine = nc.vector if b_next == 0 else nc.gpsimd
                 if step == 0:
@@ -300,29 +341,33 @@ def tile_xmem_pa_t_kernel(
                     scale_queries(b_next, engine)
                 if step == 3:
                     scale_shrinkage(b_next, engine)
-                if step == 4:
-                    channel_sums(b_next)
+            normalise_and_store((s - 12) // V_TILES, (s - 12) % V_TILES)
 
-            similarities(s + 2)
-            negated_similarities(s + 1)
-            exponentials(s)
-            regroup_e(s - 1)
-            regroup_values(s // ROW_TILES, s % ROW_TILES)
-            h, j = divmod(s - 6, V_TILES)
-            if 0 <= h < HALVES:
-                if j == 0:
-                    keep_reciprocals(h)
-                multiply_values(h, j)
-            turn_e(s)
-            if s % HALF_TILES == 1 and 0 <= (s - 5) // HALF_TILES < HALVES:
-                spread_reciprocals((s - 5) // HALF_TILES)
-            turn_values((s + 1) // ROW_TILES, (s + 1) % ROW_TILES)
-
-            if b_next < BATCH and step == 4:
+            negated_similarities(s - 1, 0)
+            negated_maximum(s - 2)
+            negated_similarities(s - 1, 1)
+            if step == 6:
                 keep_channel_sums(b_next)
-            if s % HALF_TILES == 0 and 0 <= (s - 4) // HALF_TILES < HALVES:
-                reciprocals((s - 4) // HALF_TILES)
-            if s % HALF_TILES == 1 and 0 <= (s - 5) // HALF_TILES < HALVES:
-                quantise_e((s - 5) // HALF_TILES)
-            if s % ROW_TILES == 4 and 0 <= s // ROW_TILES < BATCH:
-                quantise_values(s // ROW_TILES)
+            if quarter == 3:
+                reciprocals(h_now - 1)
+            if quarter == 1:
+                quantise_e(h_now - 2)
+            if step == 7:
+                quantise_values(b_next - 1)
+
+            regroup_e(s - 5)
+            regroup_values((s - 2) // ROW_TILES, (s - 2) % ROW_TILES)
+            leave_psum((s - 11) // V_TILES, (s - 11) % V_TILES)
+            if quarter == 1:
+                keep_reciprocals(h_now - 2)
+            exponentials(s - 3)
+
+            similarities(s, 0)
+            turn_e(s - 4)
+            similarities(s, 1)
+            turn_values((s - 1) // ROW_TILES, (s - 1) % ROW_TILES)
+            if step == 5:
+                channel_sums(b_next)
+            if quarter == 0:
+                spread_reciprocals(h_now - 2)
+            multiply_values((s - 10) // V_TILES, (s - 10) % V_TILES)

@@ -28,7 +28,7 @@ V_TILES = VALUES // P
 TILES = BATCH * ROW_TILES
 HALVES = TILES // HALF_TILES
 
-VECTOR_HALVES = 2
+VECTOR_HALVES = 3
 
 FLOPS = 2 * BATCH * (2 * P * SLOTS * PIXELS + VALUES * SLOTS * PIXELS)
 
@@ -64,11 +64,6 @@ def tile_xmem_pa_t_kernel(
             nc.sync.dma_start(out=qk[:], in_=query_key[b].rearrange("c h w -> c (h w)"))
             qe = inputs.tile([P, PIXELS], BF16)
             nc.sync.dma_start(out=qe[:], in_=query_selection[b].rearrange("c h w -> c (h w)"))
-            ms_rows = inputs.tile([P, SLOTS], BF16)
-            nc.scalar.dma_start(
-                out=ms_rows[:],
-                in_=memory_shrinkage[b].rearrange("a t h w -> (a t h w)").partition_broadcast(P),
-            )
             qs = inputs.tile([P, PIXELS], BF16)
             nc.sync.dma_start(out=qs[:], in_=qk_sel[b].rearrange("c h w -> c (h w)"))
             mk = inputs.tile([P, SLOTS], BF16)
@@ -82,13 +77,21 @@ def tile_xmem_pa_t_kernel(
                     "(j q) n -> q j n", q=P
                 ),
             )
-            live["qk", b], live["qe", b], live["ms_rows", b], live["qs", b] = qk, qe, ms_rows, qs
+            live["qk", b], live["qe", b], live["qs", b] = qk, qe, qs
             live["mk", b], live["m2", b], live["mv", b] = mk, m2, mv
 
         ident = consts.tile([P, P], F32)
         make_identity(nc, ident[:])
         ones_column = consts.tile([P, 1], F32)
         nc.gpsimd.memset(ones_column[:], 1.0)
+
+        def load_shrinkage(b):
+            ms_rows = prep.tile([P, SLOTS], BF16)
+            nc.gpsimd.dma_start(
+                out=ms_rows[:],
+                in_=memory_shrinkage[b].rearrange("a t h w -> (a t h w)").partition_broadcast(P),
+            )
+            live["ms_rows", b] = ms_rows
 
         def square_keys(b, engine):
             weighted = prep.tile([P, PIXELS], F32)
@@ -334,6 +337,7 @@ def tile_xmem_pa_t_kernel(
             if b_next < BATCH:
                 engine = nc.vector if b_next == 0 else nc.gpsimd
                 if step == 0:
+                    load_shrinkage(b_next)
                     square_keys(b_next, engine)
                 if step == 1:
                     weight_squares(b_next, engine)
@@ -346,7 +350,7 @@ def tile_xmem_pa_t_kernel(
             negated_similarities(s - 1, 0)
             negated_maximum(s - 2)
             negated_similarities(s - 1, 1)
-            if step == 6:
+            if step == 7:
                 keep_channel_sums(b_next)
             if quarter == 3:
                 reciprocals(h_now - 1)
@@ -366,7 +370,7 @@ def tile_xmem_pa_t_kernel(
             turn_e(s - 4)
             similarities(s, 1)
             turn_values((s - 1) // ROW_TILES, (s - 1) % ROW_TILES)
-            if step == 5:
+            if step == 6:
                 channel_sums(b_next)
             if quarter == 0:
                 spread_reciprocals(h_now - 2)

@@ -27,7 +27,7 @@ HALF_TILES = BANK // P
 V_TILES = VALUES // P
 TILES = BATCH * ROW_TILES
 HALVES = TILES // HALF_TILES
-
+V_UNITS = V_TILES * PASSES
 VECTOR_HALVES = 3
 
 FLOPS = 2 * BATCH * (2 * P * SLOTS * PIXELS + VALUES * SLOTS * PIXELS)
@@ -50,10 +50,11 @@ def tile_xmem_pa_t_kernel(
         inputs = ctx.enter_context(tc.tile_pool(name="inputs", bufs=BATCH))
         prep = ctx.enter_context(tc.tile_pool(name="prep", bufs=2))
         rows = ctx.enter_context(tc.tile_pool(name="rows", bufs=4))
+        groups = ctx.enter_context(tc.tile_pool(name="groups", bufs=3))
         halves = ctx.enter_context(tc.tile_pool(name="halves", bufs=2))
         results = ctx.enter_context(tc.tile_pool(name="results", bufs=6))
-        psum_wide = ctx.enter_context(tc.psum_pool(name="psum_wide", bufs=5))
-        psum_turn = ctx.enter_context(tc.psum_pool(name="psum_turn", bufs=2))
+        psum_wide = ctx.enter_context(tc.psum_pool(name="psum_wide", bufs=4))
+        psum_turn = ctx.enter_context(tc.psum_pool(name="psum_turn", bufs=3))
         psum_misc = ctx.enter_context(tc.psum_pool(name="psum_misc", bufs=1))
         ctx.enter_context(tc.manual_schedule())
 
@@ -66,6 +67,13 @@ def tile_xmem_pa_t_kernel(
             nc.sync.dma_start(out=qe[:], in_=query_selection[b].rearrange("c h w -> c (h w)"))
             qs = inputs.tile([P, PIXELS], BF16)
             nc.sync.dma_start(out=qs[:], in_=qk_sel[b].rearrange("c h w -> c (h w)"))
+            ms_rows = inputs.tile([P, SLOTS], BF16)
+            queue = nc.scalar if b == 0 else nc.sync
+            queue.dma_start(
+                out=ms_rows[:],
+                in_=memory_shrinkage[b].rearrange("a t h w -> (a t h w)").partition_broadcast(P),
+            )
+            live["ms_rows", b] = ms_rows
             mk = inputs.tile([P, SLOTS], BF16)
             nc.sync.dma_start(out=mk[:], in_=memory_key[b].rearrange("c t h w -> c (t h w)"))
             m2 = inputs.tile([P, SLOTS], BF16)
@@ -85,99 +93,97 @@ def tile_xmem_pa_t_kernel(
         ones_column = consts.tile([P, 1], F32)
         nc.gpsimd.memset(ones_column[:], 1.0)
 
-        def load_shrinkage(b):
-            ms_rows = prep.tile([P, SLOTS], BF16)
-            nc.gpsimd.dma_start(
-                out=ms_rows[:],
-                in_=memory_shrinkage[b].rearrange("a t h w -> (a t h w)").partition_broadcast(P),
-            )
-            live["ms_rows", b] = ms_rows
+        def square_keys(h, engine):
+            b, half = divmod(h, 2)
+            cols = slice(half * BANK, (half + 1) * BANK)
+            weighted = prep.tile([P, BANK], F32, bufs=3)
+            engine.tensor_tensor(out=weighted[:], in0=live["qk", b][:, cols], in1=live["qk", b][:, cols], op=ALU.mult)
+            live["weighted", h] = weighted
 
-        def square_keys(b, engine):
-            weighted = prep.tile([P, PIXELS], F32)
-            engine.tensor_tensor(out=weighted[:], in0=live["qk", b][:], in1=live["qk", b][:], op=ALU.mult)
-            live["weighted", b] = weighted
-
-        def weight_squares(b, engine):
-            weighted = live["weighted", b]
-            engine.tensor_tensor(out=weighted[:], in0=weighted[:], in1=live["qe", b][:], op=ALU.mult)
+        def weight_squares(h, engine):
+            b, half = divmod(h, 2)
+            cols = slice(half * BANK, (half + 1) * BANK)
+            weighted = live["weighted", h]
+            engine.tensor_tensor(out=weighted[:], in0=weighted[:], in1=live["qe", b][:, cols], op=ALU.mult)
 
         def scale_queries(b, engine):
-            qs2 = prep.tile([P, PIXELS], BF16)
+            qs_scaled = prep.tile([P, PIXELS], BF16)
             engine.tensor_scalar(
-                out=qs2[:], in0=live["qs", b][:], scalar1=2.0, scalar2=0.0, op0=ALU.mult, op1=ALU.add
+                out=qs_scaled[:], in0=live["qs", b][:], scalar1=-2.0, scalar2=0.0, op0=ALU.mult, op1=ALU.add
             )
-            qe_neg = prep.tile([P, PIXELS], BF16)
-            engine.tensor_scalar(
-                out=qe_neg[:], in0=live["qe", b][:], scalar1=-1.0, scalar2=0.0, op0=ALU.mult, op1=ALU.add
-            )
-            live["qs2", b], live["qe_neg", b] = qs2, qe_neg
+            live["qs_scaled", b] = qs_scaled
 
         def scale_shrinkage(b, engine):
-            neg_ms = prep.tile([P, SLOTS], F32)
+            ms_scaled = prep.tile([P, SLOTS], F32)
             engine.tensor_scalar(
-                out=neg_ms[:], in0=live["ms_rows", b][:], scalar1=-1.0 / math.sqrt(P), scalar2=0.0,
+                out=ms_scaled[:], in0=live["ms_rows", b][:], scalar1=1.0 / math.sqrt(P), scalar2=0.0,
                 op0=ALU.mult, op1=ALU.add,
             )
-            live["neg_ms", b] = neg_ms
+            live["ms_scaled", b] = ms_scaled
 
-        def channel_sums(b):
-            if not 0 <= b < BATCH:
+        def channel_sums(h):
+            if not 0 <= h < HALVES:
                 return
-            b_sq_psum = psum_misc.tile([P, ROW_TILES], F32, tag="misc")
-            for i in range(ROW_TILES):
+            b_sq_psum = psum_misc.tile([P, HALF_TILES], F32, tag="misc")
+            for j in range(HALF_TILES):
                 nc.tensor.matmul(
-                    out=b_sq_psum[:, i : i + 1], lhsT=live["weighted", b][:, i * P : (i + 1) * P],
+                    out=b_sq_psum[:, j : j + 1], lhsT=live["weighted", h][:, j * P : (j + 1) * P],
                     rhs=ones_column[:], start=True, stop=True,
                 )
-            live["b_sq_psum", b] = b_sq_psum
+            live["b_sq_psum", h] = b_sq_psum
 
-        def keep_channel_sums(b):
-            if not 0 <= b < BATCH:
+        def keep_channel_sums(h):
+            if not 0 <= h < HALVES:
                 return
-            b_sq = prep.tile([P, ROW_TILES], F32)
-            nc.vector.tensor_copy(out=b_sq[:], in_=live["b_sq_psum", b][:])
-            live["b_sq", b] = b_sq
+            b_sq = halves.tile([P, HALF_TILES], F32)
+            nc.vector.tensor_copy(out=b_sq[:], in_=live["b_sq_psum", h][:])
+            live["b_sq", h] = b_sq
 
-        def turn_words(rows_bf16, turned):
+        def turn_words(rows_bf16, turned, first_pass, passes):
             words = rows_bf16.bitcast(F32)
-            for k in range(PASSES * 2):
+            for k in range(2 * passes):
+                block = 2 * first_pass + k
                 nc.tensor.transpose(
-                    out=turned[:, k, :], in_=words[:, k * P : (k + 1) * P], identity=ident[:]
+                    out=turned[:, k, :], in_=words[:, block * P : (block + 1) * P], identity=ident[:]
                 )
 
-        def regroup_words(turned, grouped, first_col):
+        def regroup_words(turned, grouped, passes):
             nc.scalar.copy(
-                out=grouped[:].bitcast(F32).rearrange("q (g r u) -> q g r u", g=PASSES, u=2)[
-                    :, :, first_col : first_col + P, :
-                ],
-                in_=turned[:].rearrange("q (g u) r -> q g r u", g=PASSES),
+                out=grouped.bitcast(F32).rearrange("q (g r u) -> q g r u", g=passes, u=2),
+                in_=turned[:].rearrange("q (g u) r -> q g r u", g=passes),
             )
 
-        def turn_values(b, j):
-            if not (0 <= b < BATCH and j < V_TILES):
-                return
-            mv_turned = psum_turn.tile([P, PASSES * 2, P], F32, tag="turned")
-            turn_words(live["mv", b][:, j, :], mv_turned)
-            live["mv_turned", b, j] = mv_turned
+        def quantise_columns(grouped_cols, codes, scales, cols):
+            nc.vector.quantize_mx(out=codes[:, cols].bitcast(FP8X4), scales=scales[:, cols], in_=grouped_cols)
 
-        def regroup_values(b, j):
-            if not (0 <= b < BATCH and j < V_TILES):
-                return
-            if j == 0:
-                mv_grouped = prep.tile([P, PASSES * VALUES * PACK], BF16, align_bytes=64, bufs=1)
-                live["mv_grouped", b] = mv_grouped
-            regroup_words(live["mv_turned", b, j], live["mv_grouped", b], j * P)
-
-        def quantise_values(b):
+        def turn_values(b, unit):
             if not 0 <= b < BATCH:
                 return
-            mv_codes = prep.tile([P, PASSES * VALUES], U32, align_bytes=64)
-            mv_scales = prep.tile([P, PASSES * VALUES], U8, align_bytes=64)
-            nc.vector.quantize_mx(
-                out=mv_codes[:].bitcast(FP8X4), scales=mv_scales[:], in_=live["mv_grouped", b][:]
+            j, g = divmod(unit, PASSES)
+            mv_turned = psum_turn.tile([P, 2, P], F32, tag="turned")
+            turn_words(live["mv", b][:, j, :], mv_turned, g, 1)
+            live["mv_turned", b, unit] = mv_turned
+
+        def regroup_values(b, unit):
+            if not 0 <= b < BATCH:
+                return
+            first, k = divmod(unit, V_UNITS // 2)
+            if k == 0:
+                mv_grouped = groups.tile([P, V_UNITS // 2, P * PACK], BF16, align_bytes=64, bufs=2)
+                live["mv_grouped", b, first] = mv_grouped
+            regroup_words(live["mv_turned", b, unit], live["mv_grouped", b, first][:, k, :], 1)
+
+        def quantise_values(b, first):
+            if not 0 <= b < BATCH:
+                return
+            if first == 0:
+                mv_codes = prep.tile([P, V_UNITS * P], U32, align_bytes=64)
+                mv_scales = prep.tile([P, V_UNITS * P], U8, align_bytes=64)
+                live["mv_codes", b], live["mv_scales", b] = mv_codes, mv_scales
+            quantise_columns(
+                live["mv_grouped", b, first][:].rearrange("q k c -> q (k c)"), live["mv_codes", b], live["mv_scales", b],
+                slice(first * VALUES, (first + 1) * VALUES),
             )
-            live["mv_codes", b], live["mv_scales", b] = mv_codes, mv_scales
 
         def similarities(i, c):
             if not 0 <= i < TILES:
@@ -187,24 +193,24 @@ def tile_xmem_pa_t_kernel(
             cols = slice(c * BANK, (c + 1) * BANK)
             dots = psum_wide.tile([P, BANK], F32, tag="wide")
             nc.tensor.matmul(
-                out=dots[:], lhsT=live["qs2", b][:, pix], rhs=live["mk", b][:, cols], start=True, stop=False
+                out=dots[:], lhsT=live["qs_scaled", b][:, pix], rhs=live["mk", b][:, cols], start=True, stop=False
             )
             nc.tensor.matmul(
-                out=dots[:], lhsT=live["qe_neg", b][:, pix], rhs=live["m2", b][:, cols], start=False, stop=True
+                out=dots[:], lhsT=live["qe", b][:, pix], rhs=live["m2", b][:, cols], start=False, stop=True
             )
             live["dots", i, c] = dots
 
         def negated_similarities(i, c):
             if not 0 <= i < TILES:
                 return
-            b, t = divmod(i, ROW_TILES)
+            h, j = divmod(i, HALF_TILES)
             cols = slice(c * BANK, (c + 1) * BANK)
             if c == 0:
                 neg_sim = rows.tile([P, SLOTS], F32)
                 live["neg_sim", i] = neg_sim
             nc.vector.scalar_tensor_tensor(
-                out=live["neg_sim", i][:, cols], in0=live["dots", i, c][:], scalar=live["b_sq", b][:, t : t + 1],
-                in1=live["neg_ms", b][:, cols], op0=ALU.subtract, op1=ALU.mult,
+                out=live["neg_sim", i][:, cols], in0=live["dots", i, c][:], scalar=live["b_sq", h][:, j : j + 1],
+                in1=live["ms_scaled", i // ROW_TILES][:, cols], op0=ALU.add, op1=ALU.mult,
             )
 
         def negated_maximum(i):
@@ -231,8 +237,8 @@ def tile_xmem_pa_t_kernel(
         def turn_e(i):
             if not 0 <= i < TILES:
                 return
-            e_turned = psum_turn.tile([P, PASSES * 2, P], F32, tag="turned")
-            turn_words(live["e_rows", i][:], e_turned)
+            e_turned = psum_turn.tile([P, 2 * PASSES, P], F32, tag="turned")
+            turn_words(live["e_rows", i][:], e_turned, 0, PASSES)
             live["e_turned", i] = e_turned
 
         def regroup_e(i):
@@ -240,9 +246,22 @@ def tile_xmem_pa_t_kernel(
                 return
             h, j = divmod(i, HALF_TILES)
             if j == 0:
-                e_grouped = halves.tile([P, PASSES * BANK * PACK], BF16, align_bytes=64)
+                e_grouped = halves.tile([P, PASSES, BANK, PACK], BF16, align_bytes=64)
                 live["e_grouped", h] = e_grouped
-            regroup_words(live["e_turned", i], live["e_grouped", h], j * P)
+            nc.scalar.copy(
+                out=live["e_grouped", h][:].bitcast(F32)[:, :, j * P : (j + 1) * P, :],
+                in_=live["e_turned", i][:].rearrange("q (g u) r -> q g r u", g=PASSES),
+            )
+
+        def quantise_e(h):
+            if not 0 <= h < HALVES:
+                return
+            e_codes = halves.tile([P, PASSES * BANK], U32, align_bytes=64)
+            e_scales = halves.tile([P, PASSES * BANK], U8, align_bytes=64)
+            quantise_columns(
+                live["e_grouped", h][:].rearrange("q g r t -> q (g r t)"), e_codes, e_scales, slice(0, PASSES * BANK)
+            )
+            live["e_codes", h], live["e_scales", h] = e_codes, e_scales
 
         def reciprocals(h):
             if not 0 <= h < HALVES:
@@ -251,19 +270,20 @@ def tile_xmem_pa_t_kernel(
             nc.vector.reciprocal(out=recip[:], in_=live["sums", h][:])
             live["recip", h] = recip
 
-        def spread_reciprocals(h):
+        def spread_reciprocals(h, part):
             if not 0 <= h < HALVES:
                 return
-            recip_spread = psum_misc.tile([P, BANK], F32, tag="misc")
-            for j in range(HALF_TILES):
+            if part == 0:
+                recip_spread = psum_misc.tile([P, BANK], F32, tag="misc")
+                live["recip_spread", h] = recip_spread
+            for j in (2 * part, 2 * part + 1):
                 nc.tensor.matmul(
-                    out=recip_spread[:, j * P : (j + 1) * P],
+                    out=live["recip_spread", h][:, j * P : (j + 1) * P],
                     lhsT=live["recip", h][:, j : j + 1].to_broadcast([P, P]),
                     rhs=ident[:],
                     start=True,
                     stop=True,
                 )
-            live["recip_spread", h] = recip_spread
 
         def keep_reciprocals(h):
             if not 0 <= h < HALVES:
@@ -272,23 +292,13 @@ def tile_xmem_pa_t_kernel(
             nc.scalar.copy(out=recip_rows[:], in_=live["recip_spread", h][:])
             live["recip_rows", h] = recip_rows
 
-        def quantise_e(h):
-            if not 0 <= h < HALVES:
-                return
-            e_codes = halves.tile([P, PASSES * BANK], U32, align_bytes=64)
-            e_scales = halves.tile([P, PASSES * BANK], U8, align_bytes=64)
-            nc.vector.quantize_mx(
-                out=e_codes[:].bitcast(FP8X4), scales=e_scales[:], in_=live["e_grouped", h][:]
-            )
-            live["e_codes", h], live["e_scales", h] = e_codes, e_scales
-
         def multiply_values(h, j):
             if not 0 <= h < HALVES:
                 return
             b = h // 2
             acc = psum_wide.tile([P, BANK], F32, tag="wide")
             for g in range(PASSES):
-                v_cols = slice(g * VALUES + j * P, g * VALUES + (j + 1) * P)
+                v_cols = slice((j * PASSES + g) * P, (j * PASSES + g + 1) * P)
                 p_cols = slice(g * BANK, (g + 1) * BANK)
                 nc.tensor.matmul_mx(
                     out=acc[:],
@@ -330,48 +340,52 @@ def tile_xmem_pa_t_kernel(
             nc.gpsimd.tensor_tensor(out=result[:], in0=result[:], in1=live["recip_rows", h][:], op=ALU.mult)
             store(h, j, result)
 
-        for s in range(-ROW_TILES, TILES + 11):
+        for s in range(-ROW_TILES, TILES + 12):
             b_next, step = divmod(s + ROW_TILES, ROW_TILES)
             h_now, quarter = divmod(s, HALF_TILES)
 
             if b_next < BATCH:
                 engine = nc.vector if b_next == 0 else nc.gpsimd
                 if step == 0:
-                    load_shrinkage(b_next)
-                    square_keys(b_next, engine)
+                    square_keys(2 * b_next, engine)
                 if step == 1:
-                    weight_squares(b_next, engine)
+                    weight_squares(2 * b_next, engine)
                 if step == 2:
                     scale_queries(b_next, engine)
                 if step == 3:
                     scale_shrinkage(b_next, engine)
-            normalise_and_store((s - 12) // V_TILES, (s - 12) % V_TILES)
+                if step == 4:
+                    square_keys(2 * b_next + 1, nc.gpsimd)
+                if step == 5:
+                    weight_squares(2 * b_next + 1, nc.gpsimd)
+            normalise_and_store((s - 13) // V_TILES, (s - 13) % V_TILES)
 
             negated_similarities(s - 1, 0)
             negated_maximum(s - 2)
             negated_similarities(s - 1, 1)
-            if step == 7:
-                keep_channel_sums(b_next)
-            if quarter == 3:
-                reciprocals(h_now - 1)
-            if quarter == 1:
+            if quarter == 2:
                 quantise_e(h_now - 2)
-            if step == 7:
-                quantise_values(b_next - 1)
+            if quarter == 3:
+                keep_channel_sums(h_now + 1)
+                reciprocals(h_now - 1)
+            if quarter == 0:
+                quantise_values((s - 8) // V_UNITS, ((s - 8) % V_UNITS) // HALF_TILES)
 
-            regroup_e(s - 5)
-            regroup_values((s - 2) // ROW_TILES, (s - 2) % ROW_TILES)
-            leave_psum((s - 11) // V_TILES, (s - 11) % V_TILES)
-            if quarter == 1:
-                keep_reciprocals(h_now - 2)
             exponentials(s - 3)
+            if quarter == 2:
+                keep_reciprocals(h_now - 2)
+            regroup_e(s - 5)
+            regroup_values((s - 2) // V_UNITS, (s - 2) % V_UNITS)
+            leave_psum((s - 12) // V_TILES, (s - 12) % V_TILES)
 
             similarities(s, 0)
             turn_e(s - 4)
             similarities(s, 1)
-            turn_values((s - 1) // ROW_TILES, (s - 1) % ROW_TILES)
-            if step == 6:
-                channel_sums(b_next)
+            turn_values((s - 1) // V_UNITS, (s - 1) % V_UNITS)
             if quarter == 0:
-                spread_reciprocals(h_now - 2)
-            multiply_values((s - 10) // V_TILES, (s - 10) % V_TILES)
+                spread_reciprocals(h_now - 2, 0)
+            if quarter == 1:
+                spread_reciprocals(h_now - 2, 1)
+            if quarter == 2:
+                channel_sums(h_now + 1)
+            multiply_values((s - 11) // V_TILES, (s - 11) % V_TILES)

import math
from contextlib import ExitStack

import concourse.mybir as mybir
from concourse.masks import make_identity

F32 = mybir.dt.float32
BF16 = mybir.dt.bfloat16
U32 = mybir.dt.uint32
U8 = mybir.dt.uint8
FP8X4 = mybir.dt.float8_e4m3fn_x4
ALU = mybir.AluOpType
ACT = mybir.ActivationFunctionType
AXIS = mybir.AxisListType

BATCH = 4
P = 128
SLOTS = 1024
PIXELS = 1024
VALUES = 512
BANK = 512
PACK = 4
K_PASS = P * PACK
PASSES = SLOTS // K_PASS
ROW_TILES = PIXELS // P
HALF_TILES = BANK // P
V_TILES = VALUES // P
TILES = BATCH * ROW_TILES
HALVES = TILES // HALF_TILES
V_UNITS = V_TILES * PASSES
VECTOR_HALVES = 3

FLOPS = 2 * BATCH * (2 * P * SLOTS * PIXELS + VALUES * SLOTS * PIXELS)


def tile_xmem_pa_t_kernel(
    tc,
    query_key,
    query_selection,
    qk_sel,
    memory_key,
    mk_sq,
    memory_shrinkage,
    memory_value,
    out,
):
    nc = tc.nc
    with ExitStack() as ctx:
        consts = ctx.enter_context(tc.tile_pool(name="consts", bufs=1))
        inputs = ctx.enter_context(tc.tile_pool(name="inputs", bufs=BATCH))
        prep = ctx.enter_context(tc.tile_pool(name="prep", bufs=2))
        rows = ctx.enter_context(tc.tile_pool(name="rows", bufs=4))
        groups = ctx.enter_context(tc.tile_pool(name="groups", bufs=3))
        halves = ctx.enter_context(tc.tile_pool(name="halves", bufs=2))
        results = ctx.enter_context(tc.tile_pool(name="results", bufs=6))
        psum_wide = ctx.enter_context(tc.psum_pool(name="psum_wide", bufs=4))
        psum_turn = ctx.enter_context(tc.psum_pool(name="psum_turn", bufs=3))
        psum_misc = ctx.enter_context(tc.psum_pool(name="psum_misc", bufs=1))
        ctx.enter_context(tc.manual_schedule())

        live = {}

        for b in range(BATCH):
            qk = inputs.tile([P, PIXELS], BF16)
            nc.sync.dma_start(out=qk[:], in_=query_key[b].rearrange("c h w -> c (h w)"))
            qe = inputs.tile([P, PIXELS], BF16)
            nc.sync.dma_start(out=qe[:], in_=query_selection[b].rearrange("c h w -> c (h w)"))
            qs = inputs.tile([P, PIXELS], BF16)
            nc.sync.dma_start(out=qs[:], in_=qk_sel[b].rearrange("c h w -> c (h w)"))
            ms_rows = inputs.tile([P, SLOTS], BF16)
            queue = nc.scalar if b == 0 else nc.sync
            queue.dma_start(
                out=ms_rows[:],
                in_=memory_shrinkage[b].rearrange("a t h w -> (a t h w)").partition_broadcast(P),
            )
            live["ms_rows", b] = ms_rows
            mk = inputs.tile([P, SLOTS], BF16)
            nc.sync.dma_start(out=mk[:], in_=memory_key[b].rearrange("c t h w -> c (t h w)"))
            m2 = inputs.tile([P, SLOTS], BF16)
            nc.sync.dma_start(out=m2[:], in_=mk_sq[b].rearrange("c t h w -> c (t h w)"))
            mv = inputs.tile([P, V_TILES, SLOTS], BF16)
            nc.sync.dma_start(
                out=mv[:],
                in_=memory_value[b].rearrange("o c t h w -> (o c) (t h w)").rearrange(
                    "(j q) n -> q j n", q=P
                ),
            )
            live["qk", b], live["qe", b], live["qs", b] = qk, qe, qs
            live["mk", b], live["m2", b], live["mv", b] = mk, m2, mv

        ident = consts.tile([P, P], F32)
        make_identity(nc, ident[:])
        ones_column = consts.tile([P, 1], F32)
        nc.gpsimd.memset(ones_column[:], 1.0)

        def square_keys(h, engine):
            b, half = divmod(h, 2)
            cols = slice(half * BANK, (half + 1) * BANK)
            weighted = prep.tile([P, BANK], F32, bufs=3)
            engine.tensor_tensor(out=weighted[:], in0=live["qk", b][:, cols], in1=live["qk", b][:, cols], op=ALU.mult)
            live["weighted", h] = weighted

        def weight_squares(h, engine):
            b, half = divmod(h, 2)
            cols = slice(half * BANK, (half + 1) * BANK)
            weighted = live["weighted", h]
            engine.tensor_tensor(out=weighted[:], in0=weighted[:], in1=live["qe", b][:, cols], op=ALU.mult)

        def scale_queries(b, engine):
            qs_scaled = prep.tile([P, PIXELS], BF16)
            engine.tensor_scalar(
                out=qs_scaled[:], in0=live["qs", b][:], scalar1=-2.0, scalar2=0.0, op0=ALU.mult, op1=ALU.add
            )
            live["qs_scaled", b] = qs_scaled

        def scale_shrinkage(b, engine):
            ms_scaled = prep.tile([P, SLOTS], F32)
            engine.tensor_scalar(
                out=ms_scaled[:], in0=live["ms_rows", b][:], scalar1=1.0 / math.sqrt(P), scalar2=0.0,
                op0=ALU.mult, op1=ALU.add,
            )
            live["ms_scaled", b] = ms_scaled

        def channel_sums(h):
            if not 0 <= h < HALVES:
                return
            b_sq_psum = psum_misc.tile([P, HALF_TILES], F32, tag="misc")
            for j in range(HALF_TILES):
                nc.tensor.matmul(
                    out=b_sq_psum[:, j : j + 1], lhsT=live["weighted", h][:, j * P : (j + 1) * P],
                    rhs=ones_column[:], start=True, stop=True,
                )
            live["b_sq_psum", h] = b_sq_psum

        def keep_channel_sums(h):
            if not 0 <= h < HALVES:
                return
            b_sq = halves.tile([P, HALF_TILES], F32)
            nc.vector.tensor_copy(out=b_sq[:], in_=live["b_sq_psum", h][:])
            live["b_sq", h] = b_sq

        def turn_words(rows_bf16, turned, first_pass, passes):
            words = rows_bf16.bitcast(F32)
            for k in range(2 * passes):
                block = 2 * first_pass + k
                nc.tensor.transpose(
                    out=turned[:, k, :], in_=words[:, block * P : (block + 1) * P], identity=ident[:]
                )

        def regroup_words(turned, grouped, passes):
            nc.scalar.copy(
                out=grouped.bitcast(F32).rearrange("q (g r u) -> q g r u", g=passes, u=2),
                in_=turned[:].rearrange("q (g u) r -> q g r u", g=passes),
            )

        def quantise_columns(grouped_cols, codes, scales, cols):
            nc.vector.quantize_mx(out=codes[:, cols].bitcast(FP8X4), scales=scales[:, cols], in_=grouped_cols)

        def turn_values(b, unit):
            if not 0 <= b < BATCH:
                return
            j, g = divmod(unit, PASSES)
            mv_turned = psum_turn.tile([P, 2, P], F32, tag="turned")
            turn_words(live["mv", b][:, j, :], mv_turned, g, 1)
            live["mv_turned", b, unit] = mv_turned

        def regroup_values(b, unit):
            if not 0 <= b < BATCH:
                return
            first, k = divmod(unit, V_UNITS // 2)
            if k == 0:
                mv_grouped = groups.tile([P, V_UNITS // 2, P * PACK], BF16, align_bytes=64, bufs=2)
                live["mv_grouped", b, first] = mv_grouped
            regroup_words(live["mv_turned", b, unit], live["mv_grouped", b, first][:, k, :], 1)

        def quantise_values(b, first):
            if not 0 <= b < BATCH:
                return
            if first == 0:
                mv_codes = prep.tile([P, V_UNITS * P], U32, align_bytes=64)
                mv_scales = prep.tile([P, V_UNITS * P], U8, align_bytes=64)
                live["mv_codes", b], live["mv_scales", b] = mv_codes, mv_scales
            quantise_columns(
                live["mv_grouped", b, first][:].rearrange("q k c -> q (k c)"), live["mv_codes", b], live["mv_scales", b],
                slice(first * VALUES, (first + 1) * VALUES),
            )

        def similarities(i, c):
            if not 0 <= i < TILES:
                return
            b, t = divmod(i, ROW_TILES)
            pix = slice(t * P, (t + 1) * P)
            cols = slice(c * BANK, (c + 1) * BANK)
            dots = psum_wide.tile([P, BANK], F32, tag="wide")
            nc.tensor.matmul(
                out=dots[:], lhsT=live["qs_scaled", b][:, pix], rhs=live["mk", b][:, cols], start=True, stop=False
            )
            nc.tensor.matmul(
                out=dots[:], lhsT=live["qe", b][:, pix], rhs=live["m2", b][:, cols], start=False, stop=True
            )
            live["dots", i, c] = dots

        def negated_similarities(i, c):
            if not 0 <= i < TILES:
                return
            h, j = divmod(i, HALF_TILES)
            cols = slice(c * BANK, (c + 1) * BANK)
            if c == 0:
                neg_sim = rows.tile([P, SLOTS], F32)
                live["neg_sim", i] = neg_sim
            nc.vector.scalar_tensor_tensor(
                out=live["neg_sim", i][:, cols], in0=live["dots", i, c][:], scalar=live["b_sq", h][:, j : j + 1],
                in1=live["ms_scaled", i // ROW_TILES][:, cols], op0=ALU.add, op1=ALU.mult,
            )

        def negated_maximum(i):
            if not 0 <= i < TILES:
                return
            neg_max = rows.tile([P, 1], F32)
            nc.vector.tensor_reduce(out=neg_max[:], in_=live["neg_sim", i][:], axis=AXIS.X, op=ALU.min)
            live["neg_max", i] = neg_max

        def exponentials(i):
            if not 0 <= i < TILES:
                return
            h, j = divmod(i, HALF_TILES)
            if j == 0:
                sums = halves.tile([P, HALF_TILES], F32)
                live["sums", h] = sums
            e_rows = rows.tile([P, SLOTS], BF16)
            nc.scalar.activation(
                out=e_rows[:], in_=live["neg_sim", i][:], func=ACT.Exp, bias=live["neg_max", i][:], scale=-1.0,
                accum_out=live["sums", h][:, j : j + 1],
            )
            live["e_rows", i] = e_rows

        def turn_e(i):
            if not 0 <= i < TILES:
                return
            e_turned = psum_turn.tile([P, 2 * PASSES, P], F32, tag="turned")
            turn_words(live["e_rows", i][:], e_turned, 0, PASSES)
            live["e_turned", i] = e_turned

        def regroup_e(i):
            if not 0 <= i < TILES:
                return
            h, j = divmod(i, HALF_TILES)
            if j == 0:
                e_grouped = halves.tile([P, PASSES, BANK, PACK], BF16, align_bytes=64)
                live["e_grouped", h] = e_grouped
            nc.scalar.copy(
                out=live["e_grouped", h][:].bitcast(F32)[:, :, j * P : (j + 1) * P, :],
                in_=live["e_turned", i][:].rearrange("q (g u) r -> q g r u", g=PASSES),
            )

        def quantise_e(h):
            if not 0 <= h < HALVES:
                return
            e_codes = halves.tile([P, PASSES * BANK], U32, align_bytes=64)
            e_scales = halves.tile([P, PASSES * BANK], U8, align_bytes=64)
            quantise_columns(
                live["e_grouped", h][:].rearrange("q g r t -> q (g r t)"), e_codes, e_scales, slice(0, PASSES * BANK)
            )
            live["e_codes", h], live["e_scales", h] = e_codes, e_scales

        def reciprocals(h):
            if not 0 <= h < HALVES:
                return
            recip = halves.tile([P, HALF_TILES], F32)
            nc.vector.reciprocal(out=recip[:], in_=live["sums", h][:])
            live["recip", h] = recip

        def spread_reciprocals(h, part):
            if not 0 <= h < HALVES:
                return
            if part == 0:
                recip_spread = psum_misc.tile([P, BANK], F32, tag="misc")
                live["recip_spread", h] = recip_spread
            for j in (2 * part, 2 * part + 1):
                nc.tensor.matmul(
                    out=live["recip_spread", h][:, j * P : (j + 1) * P],
                    lhsT=live["recip", h][:, j : j + 1].to_broadcast([P, P]),
                    rhs=ident[:],
                    start=True,
                    stop=True,
                )

        def keep_reciprocals(h):
            if not 0 <= h < HALVES:
                return
            recip_rows = halves.tile([P, BANK], F32)
            nc.scalar.copy(out=recip_rows[:], in_=live["recip_spread", h][:])
            live["recip_rows", h] = recip_rows

        def multiply_values(h, j):
            if not 0 <= h < HALVES:
                return
            b = h // 2
            acc = psum_wide.tile([P, BANK], F32, tag="wide")
            for g in range(PASSES):
                v_cols = slice((j * PASSES + g) * P, (j * PASSES + g + 1) * P)
                p_cols = slice(g * BANK, (g + 1) * BANK)
                nc.tensor.matmul_mx(
                    out=acc[:],
                    lhsT=live["mv_codes", b][:, v_cols].bitcast(FP8X4),
                    lhsT_scale=live["mv_scales", b][:, v_cols],
                    rhs=live["e_codes", h][:, p_cols].bitcast(FP8X4),
                    rhs_scale=live["e_scales", h][:, p_cols],
                    start=(g == 0),
                    stop=(g == PASSES - 1),
                )
            live["acc", h, j] = acc

        def store(h, j, result):
            b, half = divmod(h, 2)
            nc.sync.dma_start(
                out=out[b].rearrange("o c h w -> (o c) (h w)")[
                    j * P : (j + 1) * P, half * BANK : (half + 1) * BANK
                ],
                in_=result[:],
            )

        def leave_psum(h, j):
            if not 0 <= h < HALVES:
                return
            result = results.tile([P, BANK], F32)
            if h < HALVES - VECTOR_HALVES:
                nc.scalar.copy(out=result[:], in_=live["acc", h, j][:])
                live["result", h, j] = result
            else:
                nc.vector.tensor_tensor(
                    out=result[:], in0=live["acc", h, j][:], in1=live["recip_rows", h][:], op=ALU.mult
                )
                store(h, j, result)

        def normalise_and_store(h, j):
            if not 0 <= h < HALVES - VECTOR_HALVES:
                return
            result = live["result", h, j]
            nc.gpsimd.tensor_tensor(out=result[:], in0=result[:], in1=live["recip_rows", h][:], op=ALU.mult)
            store(h, j, result)

        for s in range(-ROW_TILES, TILES + 12):
            b_next, step = divmod(s + ROW_TILES, ROW_TILES)
            h_now, quarter = divmod(s, HALF_TILES)

            if b_next < BATCH:
                engine = nc.vector if b_next == 0 else nc.gpsimd
                if step == 0:
                    square_keys(2 * b_next, engine)
                if step == 1:
                    weight_squares(2 * b_next, engine)
                if step == 2:
                    scale_queries(b_next, engine)
                if step == 3:
                    scale_shrinkage(b_next, engine)
                if step == 4:
                    square_keys(2 * b_next + 1, nc.gpsimd)
                if step == 5:
                    weight_squares(2 * b_next + 1, nc.gpsimd)
            normalise_and_store((s - 13) // V_TILES, (s - 13) % V_TILES)

            negated_similarities(s - 1, 0)
            negated_maximum(s - 2)
            negated_similarities(s - 1, 1)
            if quarter == 2:
                quantise_e(h_now - 2)
            if quarter == 3:
                keep_channel_sums(h_now + 1)
                reciprocals(h_now - 1)
            if quarter == 0:
                quantise_values((s - 8) // V_UNITS, ((s - 8) % V_UNITS) // HALF_TILES)

            exponentials(s - 3)
            if quarter == 2:
                keep_reciprocals(h_now - 2)
            regroup_e(s - 5)
            regroup_values((s - 2) // V_UNITS, (s - 2) % V_UNITS)
            leave_psum((s - 12) // V_TILES, (s - 12) % V_TILES)

            similarities(s, 0)
            turn_e(s - 4)
            similarities(s, 1)
            turn_values((s - 1) // V_UNITS, (s - 1) % V_UNITS)
            if quarter == 0:
                spread_reciprocals(h_now - 2, 0)
            if quarter == 1:
                spread_reciprocals(h_now - 2, 1)
            if quarter == 2:
                channel_sums(h_now + 1)
            multiply_values((s - 11) // V_TILES, (s - 11) % V_TILES)
